import numpy as np
import ml_dtypes


def mxq(x, axis, fmt="e4m3"):
    dtype, down = {"e4m3": (ml_dtypes.float8_e4m3fn, 7), "e5m2": (ml_dtypes.float8_e5m2, 14)}[fmt]
    v = np.moveaxis(np.asarray(x, np.float32).astype(ml_dtypes.bfloat16).astype(np.float64), axis, -1)
    blocks = v.reshape(v.shape[:-1] + (-1, 32))
    amax = np.abs(blocks).max(-1, keepdims=True)
    byte = np.maximum(np.where(amax > 0, np.frexp(amax)[1] - 1 + 127, 0) - down, 1)
    scale = np.exp2(byte - 127.0)
    codes = (blocks / scale).astype(np.float32).astype(dtype).astype(np.float64)
    return np.moveaxis((codes * scale).reshape(v.shape), -1, axis)


WIDE = False


def mx_kscale(k):
    if not WIDE:
        return np.ones(k)
    levels = np.array([10, -10, 5, -5, 0])
    if k % 512:
        return np.exp2(np.random.permutation(np.resize(levels, k // 32))).repeat(32)
    a = np.empty((k // 512, 16))
    for p in range(k // 512):
        a[p, :8] = np.random.permutation(np.resize(levels, 8))
        for g in range(8):
            far = levels[np.abs(levels - a[p, g]) >= 10]
            a[p, g + 8] = far[np.random.randint(len(far))]
    return np.exp2(a.ravel()).repeat(32)


BF16 = ml_dtypes.bfloat16


def bf(x):
    return np.asarray(x, np.float32).astype(BF16)


def f64(x):
    return np.asarray(x).astype(np.float64)


B, S, D, H = 16, 256, 512, 2


def setup_inputs():
    s = mx_kscale(D)
    t = np.tile(mx_kscale(D), H)
    return {"x": bf(np.random.standard_normal((B, S, D)) * s),
            "Wq": bf(np.random.standard_normal((D, H * D)) * 1.4 / np.sqrt(D) / s[:, None] * t),
            "Wk": bf(np.random.standard_normal((D, H * D)) * 1.4 / np.sqrt(D) / s[:, None] / t)}


def reference(x, Wq, Wk):
    xq = mxq(f64(x), 2, "e4m3")
    Q = np.reshape(xq @ mxq(f64(Wq), 0, "e4m3"), (B, H, S, D))
    K = np.reshape(xq @ mxq(f64(Wk), 0, "e4m3"), (B, H, S, D))
    scores = mxq(Q, 3, "e4m3") @ mxq(K, 3, "e4m3").transpose(0, 1, 3, 2)
    z = scores / np.sqrt(D)
    e = np.exp(z - z.max(-1, keepdims=True))
    return e / e.sum(-1, keepdims=True)

@@ -1,0 +1,281 @@
+from contextlib import ExitStack
+import math
+
+import concourse.mybir as mybir
+from concourse.masks import make_identity
+
+F32 = mybir.dt.float32
+BF16 = mybir.dt.bfloat16
+U32 = mybir.dt.uint32
+U8 = mybir.dt.uint8
+FP8X4 = mybir.dt.float8_e4m3fn_x4
+ACT = mybir.ActivationFunctionType
+AX = mybir.AxisListType
+ALU = mybir.AluOpType
+
+BATCH, SEQ, DIM, HEADS = 16, 256, 512, 2
+P = 128
+TILES = BATCH * SEQ // P
+PAIRS = TILES // 2
+SCALE = 1.0 / math.sqrt(DIM)
+FLOPS = 2 * BATCH * SEQ * DIM * 2 * HEADS * DIM + 2 * BATCH * HEADS * SEQ * SEQ * DIM
+BANK_DT = F32
+S1_BUFS = 4
+SC_BUFS = 3
+
+
+def tile_bertselfattention_pa_t_kernel(tc, x, Wq, Wk, out):
+    nc = tc.nc
+    x_rows = x.flatten_outer_dims().rearrange("(t p) k -> p t k", p=P)
+    out_rows = out.rearrange("b h (m e) j -> m (b h) (e j)", e=2)
+    weights = (Wq, Wk)
+
+    with ExitStack() as ctx:
+        const = ctx.enter_context(tc.tile_pool(name="const", bufs=1))
+        xin_pool = ctx.enter_context(tc.tile_pool(name="xin", bufs=1))
+        wprep = ctx.enter_context(tc.tile_pool(name="wprep", bufs=1))
+        work = ctx.enter_context(tc.tile_pool(name="work", bufs=3))
+        stats = ctx.enter_context(tc.tile_pool(name="stats", bufs=6))
+        ps_xt = ctx.enter_context(tc.psum_pool(name="ps_xt", bufs=1))
+        ps_s1 = ctx.enter_context(tc.psum_pool(name="ps_s1", bufs=S1_BUFS))
+        ps_sc = ctx.enter_context(tc.psum_pool(name="ps_sc", bufs=SC_BUFS))
+        ctx.enter_context(tc.manual_schedule())
+
+        ident = const.tile([P, P], F32, name="ident", tag="ident")
+        make_identity(nc, ident[:])
+        zero = const.tile([P, 1], F32, name="zero", tag="zero")
+        nc.vector.memset(zero[:], 0.0)
+        warm = const.tile([P, 1], F32, name="warm", tag="warm")
+        nc.scalar.activation(out=warm[:], in_=zero[:], func=ACT.Exp)
+
+        xin = {}
+
+        def load_x(first, count):
+            t = xin_pool.tile([P, count, DIM], BF16, name="xin%d" % first, tag="xin%d" % first)
+            nc.sync.dma_start(out=t[:], in_=x_rows[:, first:first + count, :])
+            for a in range(count):
+                xin[first + a] = t[:, a, :]
+
+        w_raw = {}
+
+        def load_w(mat, e):
+            t = wprep.tile([P, 4, DIM], BF16, name="wraw%d%d" % (mat, e), tag="wraw%d%d" % (mat, e))
+            nc.sync.dma_start(
+                out=t[:],
+                in_=weights[mat][:, e * DIM:(e + 1) * DIM].rearrange("(p j) c -> p j c", j=4),
+            )
+            w_raw[(mat, e)] = t
+
+        load_w(0, 0)
+        load_x(0, 2)
+        load_w(1, 0)
+        load_w(0, 1)
+        load_w(1, 1)
+        load_x(2, 2)
+        for first in range(4, TILES, 4):
+            load_x(first, 4)
+
+        xt_of = {}
+        gx_of = {}
+        xq_of = {}
+
+        def x_transpose(u):
+            if u < 0 or u >= PAIRS:
+                return
+            xt = ps_xt.tile([P, 2, 2, P], F32, name="xt", tag="xt")
+            for a in range(2):
+                words = xin[2 * u + a].bitcast(F32)
+                for h in range(2):
+                    nc.tensor.transpose(xt[:, a, h, :], words[:, h:DIM // 2:2], ident[:])
+            xt_of[u] = xt
+
+        def x_copy(u):
+            if u < 0 or u >= PAIRS:
+                return
+            gx = work.tile([P, 2 * P * 4], BF16, name="gx", tag="gx", align_bytes=64)
+            dst = gx[:].bitcast(F32).rearrange("p (a r h) -> p a r h", a=2, h=2)
+            src = xt_of[u][:].rearrange("p a h r -> p a r h")
+            if True:
+                nc.vector.tensor_copy(out=dst, in_=src)
+            else:
+                nc.scalar.copy(out=dst, in_=src)
+            gx_of[u] = gx
+
+        def x_quantize(u):
+            if u < 0 or u >= PAIRS:
+                return
+            xc = work.tile([P, 2 * P], U32, name="xc", tag="xc", align_bytes=64)
+            xs = work.tile([P, 2 * P], U8, name="xs", tag="xs", align_bytes=64)
+            nc.vector.quantize_mx(out=xc[:].bitcast(FP8X4), scales=xs[:], in_=gx_of[u][:])
+            xq_of[u] = (xc, xs)
+
+        w_g = {}
+        w_q = {}
+
+        def w_interleave(mat, e, engine):
+            if (mat, e) not in w_g:
+                g_new = wprep.tile(
+                    [P, 4 * DIM], BF16, name="wg%d%d" % (mat, e), tag="wg%d%d" % (mat, e), align_bytes=64
+                )
+                w_g[(mat, e)] = g_new
+            dst = w_g[(mat, e)][:].rearrange("p (t m j) -> p t m j", t=4, j=4)
+            src = w_raw[(mat, e)][:].rearrange("p j (m t) -> p t m j", t=4)
+            if engine == "v":
+                nc.vector.tensor_copy(out=dst[:, 0:2], in_=src[:, 0:2])
+            else:
+                nc.scalar.copy(out=dst[:, 2:4], in_=src[:, 2:4])
+
+        def w_quantize(mat, e):
+            wc = wprep.tile([P, DIM], U32, name="wc%d%d" % (mat, e), tag="wc%d%d" % (mat, e), align_bytes=64)
+            ws = wprep.tile([P, DIM], U8, name="ws%d%d" % (mat, e), tag="ws%d%d" % (mat, e), align_bytes=64)
+            nc.vector.quantize_mx(out=wc[:].bitcast(FP8X4), scales=ws[:], in_=w_g[(mat, e)][:])
+            w_q[(mat, e)] = (wc, ws)
+
+        bank_of = {}
+        g_of = {}
+        q_of = {}
+        sc_of = {}
+        nb_of = {}
+        ex_of = {}
+        sm_of = {}
+
+        def project(t, k):
+            if t < 0 or t >= TILES:
+                return
+            mat, e = k % 2, k // 2
+            wc, ws = w_q[(mat, e)]
+            xc, xs = xq_of[t // 2]
+            cols = slice((t % 2) * P, (t % 2 + 1) * P)
+            bank = ps_s1.tile([P, 4, P], BANK_DT, name="bank", tag="bank")
+            for j in range(4):
+                nc.tensor.matmul_mx(
+                    out=bank[:, j, :],
+                    lhsT=wc[:, j * P:(j + 1) * P].bitcast(FP8X4),
+                    lhsT_scale=ws[:, j * P:(j + 1) * P],
+                    rhs=xc[:, cols].bitcast(FP8X4),
+                    rhs_scale=xs[:, cols],
+                    start=True,
+                    stop=True,
+                )
+            bank_of[(t, k)] = bank
+
+        def read_bank(t, k, engine):
+            if t < 0 or t >= TILES:
+                return
+            mat, e = k % 2, k // 2
+            if t not in g_of:
+                g_new = work.tile([P, 4 * DIM], BF16, name="g", tag="g", align_bytes=64)
+                g_of[t] = g_new
+            o = (mat * 2 + e) * DIM
+            dst = g_of[t][:, o:o + DIM].rearrange("p (n j) -> p n j", j=4)
+            src = bank_of[(t, k)][:].rearrange("p j n -> p n j")
+            if engine == "v":
+                nc.vector.tensor_copy(out=dst, in_=src)
+            else:
+                nc.scalar.copy(out=dst, in_=src)
+
+        def quantize_qk(t):
+            if t < 0 or t >= TILES:
+                return
+            qc = work.tile([P, DIM], U32, name="qc", tag="qc", align_bytes=64)
+            qs = work.tile([P, DIM], U8, name="qs", tag="qs", align_bytes=64)
+            nc.vector.quantize_mx(out=qc[:].bitcast(FP8X4), scales=qs[:], in_=g_of[t][:])
+            q_of[t] = (qc, qs)
+
+        def scores(t):
+            if t < 0 or t >= TILES:
+                return
+            qc, qs = q_of[t]
+            sc = ps_sc.tile([P, 2, 2 * P], F32, name="sc", tag="sc")
+            for e in range(2):
+                nc.tensor.matmul_mx(
+                    out=sc[:, e, :],
+                    lhsT=qc[:, e * P:(e + 1) * P].bitcast(FP8X4),
+                    lhsT_scale=qs[:, e * P:(e + 1) * P],
+                    rhs=qc[:, 2 * P:4 * P].bitcast(FP8X4),
+                    rhs_scale=qs[:, 2 * P:4 * P],
+                    start=True,
+                    stop=True,
+                )
+            sc_of[t] = sc
+
+        def row_max(t):
+            if t < 0 or t >= TILES:
+                return
+            mx = stats.tile([P, 2], F32, name="mx", tag="mx")
+            nc.vector.reduce_max(out=mx[:], in_=sc_of[t][:], axis=AX.X)
+            nb = stats.tile([P, 2], F32, name="nb", tag="nb")
+            nc.gpsimd.tensor_scalar(out=nb[:], in0=mx[:], scalar1=-SCALE, scalar2=0.0, op0=ALU.mult, op1=ALU.add)
+            nb_of[t] = nb
+
+        def exponent(t):
+            if t < 0 or t >= TILES:
+                return
+            ex = work.tile([P, 2, 2 * P], F32, name="ex", tag="ex", bufs=4)
+            sm = stats.tile([P, 2], F32, name="sm", tag="sm")
+            for e in range(2):
+                nc.scalar.activation(
+                    out=ex[:, e, :].rearrange("p (n c) -> p n c", c=2),
+                    in_=sc_of[t][:, e, :].rearrange("p (c n) -> p n c", c=2),
+                    func=ACT.Exp,
+                    bias=nb_of[t][:, e:e + 1],
+                    scale=SCALE,
+                    accum_out=sm[:, e:e + 1],
+                )
+            ex_of[t] = ex
+            sm_of[t] = sm
+
+        def normalize(t):
+            if t < 0 or t >= TILES:
+                return
+            rs = stats.tile([P, 2], F32, name="rs", tag="rs")
+            nc.vector.reciprocal(out=rs[:], in_=sm_of[t][:])
+            pr = work.tile([P, 2, 2 * P], F32, name="pr", tag="pr", bufs=4)
+            for e in range(2):
+                nc.gpsimd.tensor_scalar(
+                    out=pr[:, e, :], in0=ex_of[t][:, e, :], scalar1=rs[:, e:e + 1], scalar2=0.0,
+                    op0=ALU.mult, op1=ALU.add,
+                )
+            nc.sync.dma_start(out=out_rows[:, t, :], in_=pr[:].rearrange("p e j -> p (e j)"))
+
+        x_transpose(0)
+        w_interleave(0, 0, "v")
+        w_interleave(0, 0, "s")
+        x_copy(0)
+        w_interleave(1, 0, "s")
+        w_quantize(0, 0)
+        w_interleave(1, 0, "v")
+        x_quantize(0)
+        project(0, 0)
+        w_interleave(0, 1, "s")
+        w_quantize(1, 0)
+        project(0, 1)
+        w_interleave(0, 1, "v")
+        w_interleave(1, 1, "s")
+        w_interleave(1, 1, "v")
+        w_quantize(0, 1)
+        project(0, 2)
+        x_transpose(1)
+        w_quantize(1, 1)
+        project(0, 3)
+
+        for s in range(0, TILES + 3):
+            read_bank(s, 0, "s")
+            quantize_qk(s - 1)
+            project(s + 1, 0)
+            scores(s - 1)
+            normalize(s - 3)
+            if s % 2 == 0:
+                x_copy(s // 2 + 1)
+            read_bank(s, 1, "s")
+            read_bank(s, 2, "v")
+            project(s + 1, 1)
+            project(s + 1, 2)
+            read_bank(s, 3, "s")
+            project(s + 1, 3)
+            row_max(s - 1)
+            exponent(s - 2)
+            if s % 2 == 0:
+                x_quantize(s // 2 + 1)
+            else:
+                x_transpose((s + 3) // 2)

@@ -20,8 +20,8 @@ PAIRS = TILES // 2
 SCALE = 1.0 / math.sqrt(DIM)
 FLOPS = 2 * BATCH * SEQ * DIM * 2 * HEADS * DIM + 2 * BATCH * HEADS * SEQ * SEQ * DIM
 BANK_DT = F32
-S1_BUFS = 4
-SC_BUFS = 3
+S1_BUFS = 5
+SC_BUFS = 2
 
 
 def tile_bertselfattention_pa_t_kernel(tc, x, Wq, Wk, out):
@@ -260,20 +260,20 @@ def tile_bertselfattention_pa_t_kernel(tc, x, Wq, Wk, out):
         project(0, 3)
 
         for s in range(0, TILES + 3):
+            row_max(s - 2)
             read_bank(s, 0, "s")
-            quantize_qk(s - 1)
             project(s + 1, 0)
-            scores(s - 1)
+            quantize_qk(s - 1)
             normalize(s - 3)
+            read_bank(s, 1, "s")
+            project(s + 1, 1)
+            scores(s - 1)
             if s % 2 == 0:
                 x_copy(s // 2 + 1)
-            read_bank(s, 1, "s")
-            read_bank(s, 2, "v")
-            project(s + 1, 1)
+            read_bank(s, 2, "s")
             project(s + 1, 2)
-            read_bank(s, 3, "s")
+            read_bank(s, 3, "v")
             project(s + 1, 3)
-            row_max(s - 1)
             exponent(s - 2)
             if s % 2 == 0:
                 x_quantize(s // 2 + 1)

from contextlib import ExitStack
import math

import concourse.mybir as mybir
from concourse.masks import make_identity

F32 = mybir.dt.float32
BF16 = mybir.dt.bfloat16
U32 = mybir.dt.uint32
U8 = mybir.dt.uint8
FP8X4 = mybir.dt.float8_e4m3fn_x4
ACT = mybir.ActivationFunctionType
AX = mybir.AxisListType
ALU = mybir.AluOpType

BATCH, SEQ, DIM, HEADS = 16, 256, 512, 2
P = 128
TILES = BATCH * SEQ // P
PAIRS = TILES // 2
SCALE = 1.0 / math.sqrt(DIM)
FLOPS = 2 * BATCH * SEQ * DIM * 2 * HEADS * DIM + 2 * BATCH * HEADS * SEQ * SEQ * DIM
BANK_DT = F32
S1_BUFS = 5
SC_BUFS = 2


def tile_bertselfattention_pa_t_kernel(tc, x, Wq, Wk, out):
    nc = tc.nc
    x_rows = x.flatten_outer_dims().rearrange("(t p) k -> p t k", p=P)
    out_rows = out.rearrange("b h (m e) j -> m (b h) (e j)", e=2)
    weights = (Wq, Wk)

    with ExitStack() as ctx:
        const = ctx.enter_context(tc.tile_pool(name="const", bufs=1))
        xin_pool = ctx.enter_context(tc.tile_pool(name="xin", bufs=1))
        wprep = ctx.enter_context(tc.tile_pool(name="wprep", bufs=1))
        work = ctx.enter_context(tc.tile_pool(name="work", bufs=3))
        stats = ctx.enter_context(tc.tile_pool(name="stats", bufs=6))
        ps_xt = ctx.enter_context(tc.psum_pool(name="ps_xt", bufs=1))
        ps_s1 = ctx.enter_context(tc.psum_pool(name="ps_s1", bufs=S1_BUFS))
        ps_sc = ctx.enter_context(tc.psum_pool(name="ps_sc", bufs=SC_BUFS))
        ctx.enter_context(tc.manual_schedule())

        ident = const.tile([P, P], F32, name="ident", tag="ident")
        make_identity(nc, ident[:])
        zero = const.tile([P, 1], F32, name="zero", tag="zero")
        nc.vector.memset(zero[:], 0.0)
        warm = const.tile([P, 1], F32, name="warm", tag="warm")
        nc.scalar.activation(out=warm[:], in_=zero[:], func=ACT.Exp)

        xin = {}

        def load_x(first, count):
            t = xin_pool.tile([P, count, DIM], BF16, name="xin%d" % first, tag="xin%d" % first)
            nc.sync.dma_start(out=t[:], in_=x_rows[:, first:first + count, :])
            for a in range(count):
                xin[first + a] = t[:, a, :]

        w_raw = {}

        def load_w(mat, e):
            t = wprep.tile([P, 4, DIM], BF16, name="wraw%d%d" % (mat, e), tag="wraw%d%d" % (mat, e))
            nc.sync.dma_start(
                out=t[:],
                in_=weights[mat][:, e * DIM:(e + 1) * DIM].rearrange("(p j) c -> p j c", j=4),
            )
            w_raw[(mat, e)] = t

        load_w(0, 0)
        load_x(0, 2)
        load_w(1, 0)
        load_w(0, 1)
        load_w(1, 1)
        load_x(2, 2)
        for first in range(4, TILES, 4):
            load_x(first, 4)

        xt_of = {}
        gx_of = {}
        xq_of = {}

        def x_transpose(u):
            if u < 0 or u >= PAIRS:
                return
            xt = ps_xt.tile([P, 2, 2, P], F32, name="xt", tag="xt")
            for a in range(2):
                words = xin[2 * u + a].bitcast(F32)
                for h in range(2):
                    nc.tensor.transpose(xt[:, a, h, :], words[:, h:DIM // 2:2], ident[:])
            xt_of[u] = xt

        def x_copy(u):
            if u < 0 or u >= PAIRS:
                return
            gx = work.tile([P, 2 * P * 4], BF16, name="gx", tag="gx", align_bytes=64)
            dst = gx[:].bitcast(F32).rearrange("p (a r h) -> p a r h", a=2, h=2)
            src = xt_of[u][:].rearrange("p a h r -> p a r h")
            if True:
                nc.vector.tensor_copy(out=dst, in_=src)
            else:
                nc.scalar.copy(out=dst, in_=src)
            gx_of[u] = gx

        def x_quantize(u):
            if u < 0 or u >= PAIRS:
                return
            xc = work.tile([P, 2 * P], U32, name="xc", tag="xc", align_bytes=64)
            xs = work.tile([P, 2 * P], U8, name="xs", tag="xs", align_bytes=64)
            nc.vector.quantize_mx(out=xc[:].bitcast(FP8X4), scales=xs[:], in_=gx_of[u][:])
            xq_of[u] = (xc, xs)

        w_g = {}
        w_q = {}

        def w_interleave(mat, e, engine):
            if (mat, e) not in w_g:
                g_new = wprep.tile(
                    [P, 4 * DIM], BF16, name="wg%d%d" % (mat, e), tag="wg%d%d" % (mat, e), align_bytes=64
                )
                w_g[(mat, e)] = g_new
            dst = w_g[(mat, e)][:].rearrange("p (t m j) -> p t m j", t=4, j=4)
            src = w_raw[(mat, e)][:].rearrange("p j (m t) -> p t m j", t=4)
            if engine == "v":
                nc.vector.tensor_copy(out=dst[:, 0:2], in_=src[:, 0:2])
            else:
                nc.scalar.copy(out=dst[:, 2:4], in_=src[:, 2:4])

        def w_quantize(mat, e):
            wc = wprep.tile([P, DIM], U32, name="wc%d%d" % (mat, e), tag="wc%d%d" % (mat, e), align_bytes=64)
            ws = wprep.tile([P, DIM], U8, name="ws%d%d" % (mat, e), tag="ws%d%d" % (mat, e), align_bytes=64)
            nc.vector.quantize_mx(out=wc[:].bitcast(FP8X4), scales=ws[:], in_=w_g[(mat, e)][:])
            w_q[(mat, e)] = (wc, ws)

        bank_of = {}
        g_of = {}
        q_of = {}
        sc_of = {}
        nb_of = {}
        ex_of = {}
        sm_of = {}

        def project(t, k):
            if t < 0 or t >= TILES:
                return
            mat, e = k % 2, k // 2
            wc, ws = w_q[(mat, e)]
            xc, xs = xq_of[t // 2]
            cols = slice((t % 2) * P, (t % 2 + 1) * P)
            bank = ps_s1.tile([P, 4, P], BANK_DT, name="bank", tag="bank")
            for j in range(4):
                nc.tensor.matmul_mx(
                    out=bank[:, j, :],
                    lhsT=wc[:, j * P:(j + 1) * P].bitcast(FP8X4),
                    lhsT_scale=ws[:, j * P:(j + 1) * P],
                    rhs=xc[:, cols].bitcast(FP8X4),
                    rhs_scale=xs[:, cols],
                    start=True,
                    stop=True,
                )
            bank_of[(t, k)] = bank

        def read_bank(t, k, engine):
            if t < 0 or t >= TILES:
                return
            mat, e = k % 2, k // 2
            if t not in g_of:
                g_new = work.tile([P, 4 * DIM], BF16, name="g", tag="g", align_bytes=64)
                g_of[t] = g_new
            o = (mat * 2 + e) * DIM
            dst = g_of[t][:, o:o + DIM].rearrange("p (n j) -> p n j", j=4)
            src = bank_of[(t, k)][:].rearrange("p j n -> p n j")
            if engine == "v":
                nc.vector.tensor_copy(out=dst, in_=src)
            else:
                nc.scalar.copy(out=dst, in_=src)

        def quantize_qk(t):
            if t < 0 or t >= TILES:
                return
            qc = work.tile([P, DIM], U32, name="qc", tag="qc", align_bytes=64)
            qs = work.tile([P, DIM], U8, name="qs", tag="qs", align_bytes=64)
            nc.vector.quantize_mx(out=qc[:].bitcast(FP8X4), scales=qs[:], in_=g_of[t][:])
            q_of[t] = (qc, qs)

        def scores(t):
            if t < 0 or t >= TILES:
                return
            qc, qs = q_of[t]
            sc = ps_sc.tile([P, 2, 2 * P], F32, name="sc", tag="sc")
            for e in range(2):
                nc.tensor.matmul_mx(
                    out=sc[:, e, :],
                    lhsT=qc[:, e * P:(e + 1) * P].bitcast(FP8X4),
                    lhsT_scale=qs[:, e * P:(e + 1) * P],
                    rhs=qc[:, 2 * P:4 * P].bitcast(FP8X4),
                    rhs_scale=qs[:, 2 * P:4 * P],
                    start=True,
                    stop=True,
                )
            sc_of[t] = sc

        def row_max(t):
            if t < 0 or t >= TILES:
                return
            mx = stats.tile([P, 2], F32, name="mx", tag="mx")
            nc.vector.reduce_max(out=mx[:], in_=sc_of[t][:], axis=AX.X)
            nb = stats.tile([P, 2], F32, name="nb", tag="nb")
            nc.gpsimd.tensor_scalar(out=nb[:], in0=mx[:], scalar1=-SCALE, scalar2=0.0, op0=ALU.mult, op1=ALU.add)
            nb_of[t] = nb

        def exponent(t):
            if t < 0 or t >= TILES:
                return
            ex = work.tile([P, 2, 2 * P], F32, name="ex", tag="ex", bufs=4)
            sm = stats.tile([P, 2], F32, name="sm", tag="sm")
            for e in range(2):
                nc.scalar.activation(
                    out=ex[:, e, :].rearrange("p (n c) -> p n c", c=2),
                    in_=sc_of[t][:, e, :].rearrange("p (c n) -> p n c", c=2),
                    func=ACT.Exp,
                    bias=nb_of[t][:, e:e + 1],
                    scale=SCALE,
                    accum_out=sm[:, e:e + 1],
                )
            ex_of[t] = ex
            sm_of[t] = sm

        def normalize(t):
            if t < 0 or t >= TILES:
                return
            rs = stats.tile([P, 2], F32, name="rs", tag="rs")
            nc.vector.reciprocal(out=rs[:], in_=sm_of[t][:])
            pr = work.tile([P, 2, 2 * P], F32, name="pr", tag="pr", bufs=4)
            for e in range(2):
                nc.gpsimd.tensor_scalar(
                    out=pr[:, e, :], in0=ex_of[t][:, e, :], scalar1=rs[:, e:e + 1], scalar2=0.0,
                    op0=ALU.mult, op1=ALU.add,
                )
            nc.sync.dma_start(out=out_rows[:, t, :], in_=pr[:].rearrange("p e j -> p (e j)"))

        x_transpose(0)
        w_interleave(0, 0, "v")
        w_interleave(0, 0, "s")
        x_copy(0)
        w_interleave(1, 0, "s")
        w_quantize(0, 0)
        w_interleave(1, 0, "v")
        x_quantize(0)
        project(0, 0)
        w_interleave(0, 1, "s")
        w_quantize(1, 0)
        project(0, 1)
        w_interleave(0, 1, "v")
        w_interleave(1, 1, "s")
        w_interleave(1, 1, "v")
        w_quantize(0, 1)
        project(0, 2)
        x_transpose(1)
        w_quantize(1, 1)
        project(0, 3)

        for s in range(0, TILES + 3):
            row_max(s - 2)
            read_bank(s, 0, "s")
            project(s + 1, 0)
            quantize_qk(s - 1)
            normalize(s - 3)
            read_bank(s, 1, "s")
            project(s + 1, 1)
            scores(s - 1)
            if s % 2 == 0:
                x_copy(s // 2 + 1)
            read_bank(s, 2, "s")
            project(s + 1, 2)
            read_bank(s, 3, "v")
            project(s + 1, 3)
            exponent(s - 2)
            if s % 2 == 0:
                x_quantize(s // 2 + 1)
            else:
                x_transpose((s + 3) // 2)
